import numpy as np
import ml_dtypes

BF16 = ml_dtypes.bfloat16


def bf(x):
    return np.asarray(x, np.float32).astype(BF16)


def f32(x):
    return np.asarray(x, np.float32)


def f64(x):
    return np.asarray(x).astype(np.float64)


def striped(idx):
    return np.tile(idx.reshape(-1, 16).T, (8, 1))


C, S, N, M = 512, 256, 128, 1536


def sigmoid(v):
    return 1.0 / (1.0 + np.exp(-v))


def setup_inputs():
    return {
        "base": f32(np.random.standard_normal((C, S))),
        "msg": bf(np.random.standard_normal((C, N))),
        "h": bf(np.random.standard_normal((C, N))),
        "w_i": bf(np.random.standard_normal((C, M)) / np.sqrt(C)),
        "w_h": bf(np.random.standard_normal((C, M)) / np.sqrt(C)),
        "b_i": f32(0.5 * np.random.standard_normal((M, 1))),
        "b_hn": f32(0.5 * np.random.standard_normal((C, 1))),
        "offs": striped(np.random.permutation(S)[:N]),
    }


def reference(base, msg, h, w_i, w_h, b_i, b_hn, offs):
    idx = offs[:16].T.reshape(-1)
    i_r, i_z, i_n = np.split(f64(w_i).T @ f64(msg) + f64(b_i), M // C)
    h_r, h_z, h_n = np.split(f64(w_h).T @ f64(h), M // C)
    r = sigmoid(i_r + h_r)
    z = sigmoid(i_z + h_z)
    n = np.tanh(i_n + r * (h_n + f64(b_hn)))
    out = f64(base).copy()
    out[:, idx] = (1.0 - z) * n + z * f64(h)
    return out

@@ -1,0 +1,143 @@
+import concourse.masks as masks
+import concourse.mybir as mybir
+
+F32 = mybir.dt.float32
+BF16 = mybir.dt.bfloat16
+U16 = mybir.dt.uint16
+ADD = mybir.AluOpType.add
+MULT = mybir.AluOpType.mult
+SIGMOID = mybir.ActivationFunctionType.Sigmoid
+TANH = mybir.ActivationFunctionType.Tanh
+
+P = 128
+C = 512
+N = 128
+S = 256
+BLOCKS = C // P
+LAST = BLOCKS - 1
+WARM_COLUMNS = 512
+WARM_MATMULS = 3
+EARLY = C + 2 * P
+
+RESET, UPDATE, CANDIDATE = 0, 1, 2
+
+FLOPS = 2 * 2 * C * 3 * C * N
+
+
+def tile_graphconvolutionlayer_kernel(tc, base, msg, h, w_i, w_h, b_i, b_hn, offs, out):
+    nc = tc.nc
+    with (
+        tc.tile_pool(name="held", bufs=1) as held,
+        tc.psum_pool(name="banks", bufs=8) as banks,
+    ):
+        zeros = held.tile([P, WARM_COLUMNS], BF16, name="zeros")
+        nc.vector.memset(zeros[:], 0.0)
+        unused = banks.tile([P, WARM_COLUMNS], F32, name="unused", tag="bank")
+        for _ in range(WARM_MATMULS):
+            nc.tensor.matmul(unused[:], lhsT=zeros[:, 0:P], rhs=zeros[:], start=True, stop=True)
+
+        msg_sb = held.tile([P, BLOCKS, N], BF16, name="msg_sb")
+        nc.scalar.dma_start(msg_sb[:], msg.rearrange("(p kb) j -> p kb j", kb=BLOCKS))
+        w_i_blocks = w_i.rearrange("(p kb) m -> p kb m", kb=BLOCKS)
+        h_sb = held.tile([P, BLOCKS, N], BF16, name="h_sb")
+        nc.scalar.dma_start(h_sb[:], h.rearrange("(kb p) j -> p kb j", p=P))
+
+        bias_rows = held.tile([P, P], F32, name="bias_rows")
+        nc.vector.memset(bias_rows[:], 0.0)
+        nc.scalar.dma_start(bias_rows[0 : 3 * BLOCKS, :], b_i.rearrange("(n p) o -> n (p o)", p=P))
+        nc.scalar.dma_start(bias_rows[3 * BLOCKS : 4 * BLOCKS, :], b_hn.rearrange("(n p) o -> n (p o)", p=P))
+
+        w_i_early = []
+        w_h_early = []
+        for kb in range(BLOCKS):
+            w_i_early.append(held.tile([P, EARLY], BF16, name=f"w_i_early{kb}"))
+            nc.sync.dma_start(w_i_early[kb][:], w_i_blocks[:, kb, 0:EARLY])
+            w_h_early.append(held.tile([P, EARLY], BF16, name=f"w_h_early{kb}"))
+            nc.sync.dma_start(w_h_early[kb][:], w_h[kb * P : (kb + 1) * P, 0:EARLY])
+        w_h_n = held.tile([P, BLOCKS, C], BF16, name="w_h_n")
+        nc.sync.dma_start(w_h_n[:], w_h.rearrange("(kb p) m -> p kb m", p=P)[:, :, CANDIDATE * C : 3 * C])
+        w_i_n = held.tile([P, BLOCKS, C], BF16, name="w_i_n")
+        nc.sync.dma_start(w_i_n[:], w_i_blocks[:, :, CANDIDATE * C : 3 * C])
+        offsets = held.tile([P, N // 16], U16, name="offsets")
+        nc.sync.dma_start(offsets[:], offs)
+        windows = [held.tile([P, S], F32, name=f"window{cb}") for cb in range(BLOCKS)]
+        for cb in (0, 1):
+            nc.sync.dma_start(windows[cb][:], base[cb * P : (cb + 1) * P, :])
+        w_i_late = held.tile([P, BLOCKS, 2 * P], BF16, name="w_i_late")
+        nc.sync.dma_start(w_i_late[:], w_i_blocks[:, :, EARLY : 2 * C])
+        w_h_late = held.tile([P, BLOCKS, 2 * P], BF16, name="w_h_late")
+        nc.sync.dma_start(w_h_late[:], w_h.rearrange("(kb p) m -> p kb m", p=P)[:, :, EARLY : 2 * C])
+        for cb in (2, 3):
+            nc.sync.dma_start(windows[cb][:], base[cb * P : (cb + 1) * P, :])
+
+        def column(biases, row):
+            return biases[:, row : row + 1]
+
+        def new_bank(name):
+            return banks.tile([P, N], F32, name=name, tag="bank")
+
+        r = held.tile([P, BLOCKS, N], F32, name="r")
+        n = held.tile([P, BLOCKS, N], F32, name="n")
+        one_minus_z = held.tile([P, BLOCKS, N], F32, name="one_minus_z")
+        kept = held.tile([P, BLOCKS, N], F32, name="kept")
+
+        def update_gate(cb, sum_z):
+            z = held.tile([P, N], F32, name=f"z{cb}")
+            nc.scalar.activation(z[:], sum_z[:], SIGMOID, bias=column(bias, UPDATE * BLOCKS + cb))
+            nc.scalar.activation(
+                one_minus_z[:, cb, :], sum_z[:], SIGMOID, bias=column(minus_bias, UPDATE * BLOCKS + cb), scale=-1.0
+            )
+            nc.vector.tensor_tensor(kept[:, cb, :], z[:], h_sb[:, cb, :], MULT)
+
+        def scatter(cb):
+            fresh = held.tile([P, N], F32, name=f"fresh{cb}")
+            nc.vector.tensor_tensor(fresh[:], one_minus_z[:, cb, :], n[:, cb, :], MULT)
+            nc.vector.tensor_tensor(windows[cb][:].indirect(offsets[:]), fresh[:], kept[:, cb, :], ADD)
+            nc.sync.dma_start(out[cb * P : (cb + 1) * P, :], windows[cb][:])
+
+        early_sums = [new_bank(f"early_sum{i}") for i in range(EARLY // P)]
+        for kb in range(BLOCKS):
+            for i in range(EARLY // P):
+                nc.tensor.matmul(
+                    early_sums[i][:], lhsT=w_i_early[kb][:, i * P : (i + 1) * P], rhs=msg_sb[:, kb, :], start=kb == 0, stop=False
+                )
+            for i in range(EARLY // P):
+                nc.tensor.matmul(
+                    early_sums[i][:], lhsT=w_h_early[kb][:, i * P : (i + 1) * P], rhs=h_sb[:, kb, :], start=False, stop=kb == LAST
+                )
+        identity = held.tile([P, P], F32, name="identity")
+        masks.make_identity(nc, identity[:])
+        bias_ps = banks.tile([P, P], F32, name="bias_ps", tag="bank")
+        nc.tensor.transpose(bias_ps[:], bias_rows[:], identity[:])
+        bias = held.tile([P, 4 * BLOCKS], F32, name="bias")
+        nc.vector.tensor_copy(bias[:], bias_ps[:, 0 : 4 * BLOCKS])
+        minus_bias = held.tile([P, 4 * BLOCKS], F32, name="minus_bias")
+        nc.vector.tensor_scalar_mul(minus_bias[:], bias_ps[:, 0 : 4 * BLOCKS], -1.0)
+
+        for cb in range(BLOCKS):
+            nc.scalar.activation(r[:, cb, :], early_sums[cb][:], SIGMOID, bias=column(bias, RESET * BLOCKS + cb))
+        for cb in (0, 1):
+            update_gate(cb, early_sums[BLOCKS + cb])
+
+        for cb in range(BLOCKS):
+            e_n = new_bank(f"e_n{cb}")
+            for kb in range(BLOCKS):
+                nc.tensor.matmul(e_n[:], lhsT=w_h_n[:, kb, cb * P : (cb + 1) * P], rhs=h_sb[:, kb, :], start=kb == 0, stop=kb == LAST)
+            nc.vector.scalar_tensor_tensor(n[:, cb, :], e_n[:], column(bias, 3 * BLOCKS + cb), r[:, cb, :], op0=ADD, op1=MULT)
+        for cb in range(BLOCKS):
+            a_n = new_bank(f"a_n{cb}")
+            for kb in range(BLOCKS):
+                nc.tensor.matmul(a_n[:], lhsT=w_i_n[:, kb, cb * P : (cb + 1) * P], rhs=msg_sb[:, kb, :], start=kb == 0, stop=kb == LAST)
+            nc.vector.tensor_tensor(n[:, cb, :], n[:, cb, :], a_n[:], ADD)
+            nc.scalar.activation(n[:, cb, :], n[:, cb, :], TANH, bias=column(bias, CANDIDATE * BLOCKS + cb))
+
+        for cb in (0, 1):
+            scatter(cb)
+        for cb in (2, 3):
+            sum_z = new_bank(f"sum_z{cb}")
+            for kb in range(BLOCKS):
+                nc.tensor.matmul(sum_z[:], lhsT=w_i_late[:, kb, (cb - 2) * P : (cb - 1) * P], rhs=msg_sb[:, kb, :], start=kb == 0, stop=False)
+            for kb in range(BLOCKS):
+                nc.tensor.matmul(sum_z[:], lhsT=w_h_late[:, kb, (cb - 2) * P : (cb - 1) * P], rhs=h_sb[:, kb, :], start=False, stop=kb == LAST)
+            update_gate(cb, sum_z)
+            scatter(cb)

@@ -1,4 +1,3 @@
-import concourse.masks as masks
 import concourse.mybir as mybir
 
 F32 = mybir.dt.float32
@@ -15,11 +14,13 @@ N = 128
 S = 256
 BLOCKS = C // P
 LAST = BLOCKS - 1
+QUADRANT = 32
 WARM_COLUMNS = 512
 WARM_MATMULS = 3
 EARLY = C + 2 * P
 
 RESET, UPDATE, CANDIDATE = 0, 1, 2
+HIDDEN = 3
 
 FLOPS = 2 * 2 * C * 3 * C * N
 
@@ -42,10 +43,14 @@ def tile_graphconvolutionlayer_kernel(tc, base, msg, h, w_i, w_h, b_i, b_hn, off
         h_sb = held.tile([P, BLOCKS, N], BF16, name="h_sb")
         nc.scalar.dma_start(h_sb[:], h.rearrange("(kb p) j -> p kb j", p=P))
 
-        bias_rows = held.tile([P, P], F32, name="bias_rows")
+        bias_rows = held.tile([P, QUADRANT], F32, name="bias_rows", align_bytes=64)
         nc.vector.memset(bias_rows[:], 0.0)
-        nc.scalar.dma_start(bias_rows[0 : 3 * BLOCKS, :], b_i.rearrange("(n p) o -> n (p o)", p=P))
-        nc.scalar.dma_start(bias_rows[3 * BLOCKS : 4 * BLOCKS, :], b_hn.rearrange("(n p) o -> n (p o)", p=P))
+
+        def load_biases():
+            gates_rows = b_i[0 : 2 * C, :].rearrange("(n q i) o -> q n (i o)", q=P // QUADRANT, i=QUADRANT)
+            nc.sync.dma_start(bias_rows[0:P:4, :], gates_rows)
+            for row, vectors in ((1, b_i[2 * C : 3 * C, :]), (2, b_hn)):
+                nc.sync.dma_start(bias_rows[row:P:8, :], vectors.rearrange("(n q i) o -> q n (i o)", q=P // QUADRANT, i=QUADRANT))
 
         w_i_early = []
         w_h_early = []
@@ -54,6 +59,13 @@ def tile_graphconvolutionlayer_kernel(tc, base, msg, h, w_i, w_h, b_i, b_hn, off
             nc.sync.dma_start(w_i_early[kb][:], w_i_blocks[:, kb, 0:EARLY])
             w_h_early.append(held.tile([P, EARLY], BF16, name=f"w_h_early{kb}"))
             nc.sync.dma_start(w_h_early[kb][:], w_h[kb * P : (kb + 1) * P, 0:EARLY])
+            if kb == LAST - 1:
+                load_biases()
+
+        bias = held.tile([P, QUADRANT], F32, name="bias", align_bytes=64)
+        nc.vector.transpose(bias[:], bias_rows[:])
+        minus_bias = held.tile([P, QUADRANT], F32, name="minus_bias")
+        nc.vector.tensor_scalar_mul(minus_bias[:], bias[:], -1.0)
         w_h_n = held.tile([P, BLOCKS, C], BF16, name="w_h_n")
         nc.sync.dma_start(w_h_n[:], w_h.rearrange("(kb p) m -> p kb m", p=P)[:, :, CANDIDATE * C : 3 * C])
         w_i_n = held.tile([P, BLOCKS, C], BF16, name="w_i_n")
@@ -70,7 +82,8 @@ def tile_graphconvolutionlayer_kernel(tc, base, msg, h, w_i, w_h, b_i, b_hn, off
         for cb in (2, 3):
             nc.sync.dma_start(windows[cb][:], base[cb * P : (cb + 1) * P, :])
 
-        def column(biases, row):
+        def column(biases, gate, cb):
+            row = (gate * BLOCKS + cb) * 4 if gate < CANDIDATE else cb * 8 + gate - UPDATE
             return biases[:, row : row + 1]
 
         def new_bank(name):
@@ -83,9 +96,9 @@ def tile_graphconvolutionlayer_kernel(tc, base, msg, h, w_i, w_h, b_i, b_hn, off
 
         def update_gate(cb, sum_z):
             z = held.tile([P, N], F32, name=f"z{cb}")
-            nc.scalar.activation(z[:], sum_z[:], SIGMOID, bias=column(bias, UPDATE * BLOCKS + cb))
+            nc.scalar.activation(z[:], sum_z[:], SIGMOID, bias=column(bias, UPDATE, cb))
             nc.scalar.activation(
-                one_minus_z[:, cb, :], sum_z[:], SIGMOID, bias=column(minus_bias, UPDATE * BLOCKS + cb), scale=-1.0
+                one_minus_z[:, cb, :], sum_z[:], SIGMOID, bias=column(minus_bias, UPDATE, cb), scale=-1.0
             )
             nc.vector.tensor_tensor(kept[:, cb, :], z[:], h_sb[:, cb, :], MULT)
 
@@ -105,17 +118,8 @@ def tile_graphconvolutionlayer_kernel(tc, base, msg, h, w_i, w_h, b_i, b_hn, off
                 nc.tensor.matmul(
                     early_sums[i][:], lhsT=w_h_early[kb][:, i * P : (i + 1) * P], rhs=h_sb[:, kb, :], start=False, stop=kb == LAST
                 )
-        identity = held.tile([P, P], F32, name="identity")
-        masks.make_identity(nc, identity[:])
-        bias_ps = banks.tile([P, P], F32, name="bias_ps", tag="bank")
-        nc.tensor.transpose(bias_ps[:], bias_rows[:], identity[:])
-        bias = held.tile([P, 4 * BLOCKS], F32, name="bias")
-        nc.vector.tensor_copy(bias[:], bias_ps[:, 0 : 4 * BLOCKS])
-        minus_bias = held.tile([P, 4 * BLOCKS], F32, name="minus_bias")
-        nc.vector.tensor_scalar_mul(minus_bias[:], bias_ps[:, 0 : 4 * BLOCKS], -1.0)
-
         for cb in range(BLOCKS):
-            nc.scalar.activation(r[:, cb, :], early_sums[cb][:], SIGMOID, bias=column(bias, RESET * BLOCKS + cb))
+            nc.scalar.activation(r[:, cb, :], early_sums[cb][:], SIGMOID, bias=column(bias, RESET, cb))
         for cb in (0, 1):
             update_gate(cb, early_sums[BLOCKS + cb])
 
@@ -123,13 +127,13 @@ def tile_graphconvolutionlayer_kernel(tc, base, msg, h, w_i, w_h, b_i, b_hn, off
             e_n = new_bank(f"e_n{cb}")
             for kb in range(BLOCKS):
                 nc.tensor.matmul(e_n[:], lhsT=w_h_n[:, kb, cb * P : (cb + 1) * P], rhs=h_sb[:, kb, :], start=kb == 0, stop=kb == LAST)
-            nc.vector.scalar_tensor_tensor(n[:, cb, :], e_n[:], column(bias, 3 * BLOCKS + cb), r[:, cb, :], op0=ADD, op1=MULT)
+            nc.vector.scalar_tensor_tensor(n[:, cb, :], e_n[:], column(bias, HIDDEN, cb), r[:, cb, :], op0=ADD, op1=MULT)
         for cb in range(BLOCKS):
             a_n = new_bank(f"a_n{cb}")
             for kb in range(BLOCKS):
                 nc.tensor.matmul(a_n[:], lhsT=w_i_n[:, kb, cb * P : (cb + 1) * P], rhs=msg_sb[:, kb, :], start=kb == 0, stop=kb == LAST)
             nc.vector.tensor_tensor(n[:, cb, :], n[:, cb, :], a_n[:], ADD)
-            nc.scalar.activation(n[:, cb, :], n[:, cb, :], TANH, bias=column(bias, CANDIDATE * BLOCKS + cb))
+            nc.scalar.activation(n[:, cb, :], n[:, cb, :], TANH, bias=column(bias, CANDIDATE, cb))
 
         for cb in (0, 1):
             scatter(cb)

@@ -37,6 +37,9 @@ def tile_graphconvolutionlayer_kernel(tc, base, msg, h, w_i, w_h, b_i, b_hn, off
         for _ in range(WARM_MATMULS):
             nc.tensor.matmul(unused[:], lhsT=zeros[:, 0:P], rhs=zeros[:], start=True, stop=True)
 
+        early = held.tile([P, 1], F32, name="early")
+        nc.scalar.activation(early[:], zeros[:, 0:1], SIGMOID)
+
         msg_sb = held.tile([P, BLOCKS, N], BF16, name="msg_sb")
         nc.scalar.dma_start(msg_sb[:], msg.rearrange("(p kb) j -> p kb j", kb=BLOCKS))
         w_i_blocks = w_i.rearrange("(p kb) m -> p kb m", kb=BLOCKS)
@@ -52,34 +55,40 @@ def tile_graphconvolutionlayer_kernel(tc, base, msg, h, w_i, w_h, b_i, b_hn, off
             for row, vectors in ((1, b_i[2 * C : 3 * C, :]), (2, b_hn)):
                 nc.sync.dma_start(bias_rows[row:P:8, :], vectors.rearrange("(n q i) o -> q n (i o)", q=P // QUADRANT, i=QUADRANT))
 
+        w_h_blocks = w_h.rearrange("(kb p) m -> p kb m", p=P)
         w_i_early = []
         w_h_early = []
+
+        def load_early(early, name, blocks, count):
+            first = len(early)
+            tile = held.tile([P, count, EARLY], BF16, name=f"{name}{first}")
+            nc.sync.dma_start(tile[:], blocks[:, first : first + count, 0:EARLY])
+            early += [tile[:, i, :] for i in range(count)]
+
         for kb in range(BLOCKS):
-            w_i_early.append(held.tile([P, EARLY], BF16, name=f"w_i_early{kb}"))
-            nc.sync.dma_start(w_i_early[kb][:], w_i_blocks[:, kb, 0:EARLY])
-            w_h_early.append(held.tile([P, EARLY], BF16, name=f"w_h_early{kb}"))
-            nc.sync.dma_start(w_h_early[kb][:], w_h[kb * P : (kb + 1) * P, 0:EARLY])
-            if kb == LAST - 1:
+            if kb < LAST:
+                load_early(w_i_early, "w_i_early", w_i_blocks, 2 if kb == LAST - 1 else 1)
+            if kb == LAST:
                 load_biases()
+            load_early(w_h_early, "w_h_early", w_h_blocks, 1)
 
         bias = held.tile([P, QUADRANT], F32, name="bias", align_bytes=64)
         nc.vector.transpose(bias[:], bias_rows[:])
         minus_bias = held.tile([P, QUADRANT], F32, name="minus_bias")
         nc.vector.tensor_scalar_mul(minus_bias[:], bias[:], -1.0)
         w_h_n = held.tile([P, BLOCKS, C], BF16, name="w_h_n")
-        nc.sync.dma_start(w_h_n[:], w_h.rearrange("(kb p) m -> p kb m", p=P)[:, :, CANDIDATE * C : 3 * C])
+        nc.sync.dma_start(w_h_n[:], w_h_blocks[:, :, CANDIDATE * C : 3 * C])
         w_i_n = held.tile([P, BLOCKS, C], BF16, name="w_i_n")
         nc.sync.dma_start(w_i_n[:], w_i_blocks[:, :, CANDIDATE * C : 3 * C])
         offsets = held.tile([P, N // 16], U16, name="offsets")
         nc.sync.dma_start(offsets[:], offs)
         windows = [held.tile([P, S], F32, name=f"window{cb}") for cb in range(BLOCKS)]
-        for cb in (0, 1):
-            nc.sync.dma_start(windows[cb][:], base[cb * P : (cb + 1) * P, :])
+        nc.sync.dma_start(windows[0][:], base[0:P, :])
         w_i_late = held.tile([P, BLOCKS, 2 * P], BF16, name="w_i_late")
         nc.sync.dma_start(w_i_late[:], w_i_blocks[:, :, EARLY : 2 * C])
         w_h_late = held.tile([P, BLOCKS, 2 * P], BF16, name="w_h_late")
-        nc.sync.dma_start(w_h_late[:], w_h.rearrange("(kb p) m -> p kb m", p=P)[:, :, EARLY : 2 * C])
-        for cb in (2, 3):
+        nc.sync.dma_start(w_h_late[:], w_h_blocks[:, :, EARLY : 2 * C])
+        for cb in (1, 2, 3):
             nc.sync.dma_start(windows[cb][:], base[cb * P : (cb + 1) * P, :])
 
         def column(biases, gate, cb):
@@ -91,20 +100,16 @@ def tile_graphconvolutionlayer_kernel(tc, base, msg, h, w_i, w_h, b_i, b_hn, off
 
         r = held.tile([P, BLOCKS, N], F32, name="r")
         n = held.tile([P, BLOCKS, N], F32, name="n")
-        one_minus_z = held.tile([P, BLOCKS, N], F32, name="one_minus_z")
+        z = held.tile([P, BLOCKS, N], F32, name="z")
         kept = held.tile([P, BLOCKS, N], F32, name="kept")
 
         def update_gate(cb, sum_z):
-            z = held.tile([P, N], F32, name=f"z{cb}")
-            nc.scalar.activation(z[:], sum_z[:], SIGMOID, bias=column(bias, UPDATE, cb))
-            nc.scalar.activation(
-                one_minus_z[:, cb, :], sum_z[:], SIGMOID, bias=column(minus_bias, UPDATE, cb), scale=-1.0
-            )
-            nc.vector.tensor_tensor(kept[:, cb, :], z[:], h_sb[:, cb, :], MULT)
+            nc.scalar.activation(z[:, cb, :], sum_z[:], SIGMOID, bias=column(bias, UPDATE, cb))
+            nc.vector.tensor_tensor(kept[:, cb, :], z[:, cb, :], h_sb[:, cb, :], MULT)
 
         def scatter(cb):
             fresh = held.tile([P, N], F32, name=f"fresh{cb}")
-            nc.vector.tensor_tensor(fresh[:], one_minus_z[:, cb, :], n[:, cb, :], MULT)
+            nc.vector.scalar_tensor_tensor(fresh[:], z[:, cb, :], -1.0, n[:, cb, :], op0=ADD, op1=MULT)
             nc.vector.tensor_tensor(windows[cb][:].indirect(offsets[:]), fresh[:], kept[:, cb, :], ADD)
             nc.sync.dma_start(out[cb * P : (cb + 1) * P, :], windows[cb][:])
 
@@ -133,7 +138,7 @@ def tile_graphconvolutionlayer_kernel(tc, base, msg, h, w_i, w_h, b_i, b_hn, off
             for kb in range(BLOCKS):
                 nc.tensor.matmul(a_n[:], lhsT=w_i_n[:, kb, cb * P : (cb + 1) * P], rhs=msg_sb[:, kb, :], start=kb == 0, stop=kb == LAST)
             nc.vector.tensor_tensor(n[:, cb, :], n[:, cb, :], a_n[:], ADD)
-            nc.scalar.activation(n[:, cb, :], n[:, cb, :], TANH, bias=column(bias, CANDIDATE, cb))
+            nc.scalar.activation(n[:, cb, :], n[:, cb, :], TANH, bias=column(minus_bias, CANDIDATE, cb), scale=-1.0)
 
         for cb in (0, 1):
             scatter(cb)

import concourse.mybir as mybir

F32 = mybir.dt.float32
BF16 = mybir.dt.bfloat16
U16 = mybir.dt.uint16
ADD = mybir.AluOpType.add
MULT = mybir.AluOpType.mult
SIGMOID = mybir.ActivationFunctionType.Sigmoid
TANH = mybir.ActivationFunctionType.Tanh

P = 128
C = 512
N = 128
S = 256
BLOCKS = C // P
LAST = BLOCKS - 1
QUADRANT = 32
WARM_COLUMNS = 512
WARM_MATMULS = 3
EARLY = C + 2 * P

RESET, UPDATE, CANDIDATE = 0, 1, 2
HIDDEN = 3

FLOPS = 2 * 2 * C * 3 * C * N


def tile_graphconvolutionlayer_kernel(tc, base, msg, h, w_i, w_h, b_i, b_hn, offs, out):
    nc = tc.nc
    with (
        tc.tile_pool(name="held", bufs=1) as held,
        tc.psum_pool(name="banks", bufs=8) as banks,
    ):
        zeros = held.tile([P, WARM_COLUMNS], BF16, name="zeros")
        nc.vector.memset(zeros[:], 0.0)
        unused = banks.tile([P, WARM_COLUMNS], F32, name="unused", tag="bank")
        for _ in range(WARM_MATMULS):
            nc.tensor.matmul(unused[:], lhsT=zeros[:, 0:P], rhs=zeros[:], start=True, stop=True)

        early = held.tile([P, 1], F32, name="early")
        nc.scalar.activation(early[:], zeros[:, 0:1], SIGMOID)

        msg_sb = held.tile([P, BLOCKS, N], BF16, name="msg_sb")
        nc.scalar.dma_start(msg_sb[:], msg.rearrange("(p kb) j -> p kb j", kb=BLOCKS))
        w_i_blocks = w_i.rearrange("(p kb) m -> p kb m", kb=BLOCKS)
        h_sb = held.tile([P, BLOCKS, N], BF16, name="h_sb")
        nc.scalar.dma_start(h_sb[:], h.rearrange("(kb p) j -> p kb j", p=P))

        bias_rows = held.tile([P, QUADRANT], F32, name="bias_rows", align_bytes=64)
        nc.vector.memset(bias_rows[:], 0.0)

        def load_biases():
            gates_rows = b_i[0 : 2 * C, :].rearrange("(n q i) o -> q n (i o)", q=P // QUADRANT, i=QUADRANT)
            nc.sync.dma_start(bias_rows[0:P:4, :], gates_rows)
            for row, vectors in ((1, b_i[2 * C : 3 * C, :]), (2, b_hn)):
                nc.sync.dma_start(bias_rows[row:P:8, :], vectors.rearrange("(n q i) o -> q n (i o)", q=P // QUADRANT, i=QUADRANT))

        w_h_blocks = w_h.rearrange("(kb p) m -> p kb m", p=P)
        w_i_early = []
        w_h_early = []

        def load_early(early, name, blocks, count):
            first = len(early)
            tile = held.tile([P, count, EARLY], BF16, name=f"{name}{first}")
            nc.sync.dma_start(tile[:], blocks[:, first : first + count, 0:EARLY])
            early += [tile[:, i, :] for i in range(count)]

        for kb in range(BLOCKS):
            if kb < LAST:
                load_early(w_i_early, "w_i_early", w_i_blocks, 2 if kb == LAST - 1 else 1)
            if kb == LAST:
                load_biases()
            load_early(w_h_early, "w_h_early", w_h_blocks, 1)

        bias = held.tile([P, QUADRANT], F32, name="bias", align_bytes=64)
        nc.vector.transpose(bias[:], bias_rows[:])
        minus_bias = held.tile([P, QUADRANT], F32, name="minus_bias")
        nc.vector.tensor_scalar_mul(minus_bias[:], bias[:], -1.0)
        w_h_n = held.tile([P, BLOCKS, C], BF16, name="w_h_n")
        nc.sync.dma_start(w_h_n[:], w_h_blocks[:, :, CANDIDATE * C : 3 * C])
        w_i_n = held.tile([P, BLOCKS, C], BF16, name="w_i_n")
        nc.sync.dma_start(w_i_n[:], w_i_blocks[:, :, CANDIDATE * C : 3 * C])
        offsets = held.tile([P, N // 16], U16, name="offsets")
        nc.sync.dma_start(offsets[:], offs)
        windows = [held.tile([P, S], F32, name=f"window{cb}") for cb in range(BLOCKS)]
        nc.sync.dma_start(windows[0][:], base[0:P, :])
        w_i_late = held.tile([P, BLOCKS, 2 * P], BF16, name="w_i_late")
        nc.sync.dma_start(w_i_late[:], w_i_blocks[:, :, EARLY : 2 * C])
        w_h_late = held.tile([P, BLOCKS, 2 * P], BF16, name="w_h_late")
        nc.sync.dma_start(w_h_late[:], w_h_blocks[:, :, EARLY : 2 * C])
        for cb in (1, 2, 3):
            nc.sync.dma_start(windows[cb][:], base[cb * P : (cb + 1) * P, :])

        def column(biases, gate, cb):
            row = (gate * BLOCKS + cb) * 4 if gate < CANDIDATE else cb * 8 + gate - UPDATE
            return biases[:, row : row + 1]

        def new_bank(name):
            return banks.tile([P, N], F32, name=name, tag="bank")

        r = held.tile([P, BLOCKS, N], F32, name="r")
        n = held.tile([P, BLOCKS, N], F32, name="n")
        z = held.tile([P, BLOCKS, N], F32, name="z")
        kept = held.tile([P, BLOCKS, N], F32, name="kept")

        def update_gate(cb, sum_z):
            nc.scalar.activation(z[:, cb, :], sum_z[:], SIGMOID, bias=column(bias, UPDATE, cb))
            nc.vector.tensor_tensor(kept[:, cb, :], z[:, cb, :], h_sb[:, cb, :], MULT)

        def scatter(cb):
            fresh = held.tile([P, N], F32, name=f"fresh{cb}")
            nc.vector.scalar_tensor_tensor(fresh[:], z[:, cb, :], -1.0, n[:, cb, :], op0=ADD, op1=MULT)
            nc.vector.tensor_tensor(windows[cb][:].indirect(offsets[:]), fresh[:], kept[:, cb, :], ADD)
            nc.sync.dma_start(out[cb * P : (cb + 1) * P, :], windows[cb][:])

        early_sums = [new_bank(f"early_sum{i}") for i in range(EARLY // P)]
        for kb in range(BLOCKS):
            for i in range(EARLY // P):
                nc.tensor.matmul(
                    early_sums[i][:], lhsT=w_i_early[kb][:, i * P : (i + 1) * P], rhs=msg_sb[:, kb, :], start=kb == 0, stop=False
                )
            for i in range(EARLY // P):
                nc.tensor.matmul(
                    early_sums[i][:], lhsT=w_h_early[kb][:, i * P : (i + 1) * P], rhs=h_sb[:, kb, :], start=False, stop=kb == LAST
                )
        for cb in range(BLOCKS):
            nc.scalar.activation(r[:, cb, :], early_sums[cb][:], SIGMOID, bias=column(bias, RESET, cb))
        for cb in (0, 1):
            update_gate(cb, early_sums[BLOCKS + cb])

        for cb in range(BLOCKS):
            e_n = new_bank(f"e_n{cb}")
            for kb in range(BLOCKS):
                nc.tensor.matmul(e_n[:], lhsT=w_h_n[:, kb, cb * P : (cb + 1) * P], rhs=h_sb[:, kb, :], start=kb == 0, stop=kb == LAST)
            nc.vector.scalar_tensor_tensor(n[:, cb, :], e_n[:], column(bias, HIDDEN, cb), r[:, cb, :], op0=ADD, op1=MULT)
        for cb in range(BLOCKS):
            a_n = new_bank(f"a_n{cb}")
            for kb in range(BLOCKS):
                nc.tensor.matmul(a_n[:], lhsT=w_i_n[:, kb, cb * P : (cb + 1) * P], rhs=msg_sb[:, kb, :], start=kb == 0, stop=kb == LAST)
            nc.vector.tensor_tensor(n[:, cb, :], n[:, cb, :], a_n[:], ADD)
            nc.scalar.activation(n[:, cb, :], n[:, cb, :], TANH, bias=column(minus_bias, CANDIDATE, cb), scale=-1.0)

        for cb in (0, 1):
            scatter(cb)
        for cb in (2, 3):
            sum_z = new_bank(f"sum_z{cb}")
            for kb in range(BLOCKS):
                nc.tensor.matmul(sum_z[:], lhsT=w_i_late[:, kb, (cb - 2) * P : (cb - 1) * P], rhs=msg_sb[:, kb, :], start=kb == 0, stop=False)
            for kb in range(BLOCKS):
                nc.tensor.matmul(sum_z[:], lhsT=w_h_late[:, kb, (cb - 2) * P : (cb - 1) * P], rhs=h_sb[:, kb, :], start=False, stop=kb == LAST)
            update_gate(cb, sum_z)
            scatter(cb)
